import numpy as np
import ml_dtypes


def mxq(x, axis, fmt="e4m3"):
    dtype, down = {"e4m3": (ml_dtypes.float8_e4m3fn, 7), "e5m2": (ml_dtypes.float8_e5m2, 14)}[fmt]
    v = np.moveaxis(np.asarray(x, np.float32).astype(ml_dtypes.bfloat16).astype(np.float64), axis, -1)
    blocks = v.reshape(v.shape[:-1] + (-1, 32))
    amax = np.abs(blocks).max(-1, keepdims=True)
    byte = np.maximum(np.where(amax > 0, np.frexp(amax)[1] - 1 + 127, 0) - down, 1)
    scale = np.exp2(byte - 127.0)
    codes = (blocks / scale).astype(np.float32).astype(dtype).astype(np.float64)
    return np.moveaxis((codes * scale).reshape(v.shape), -1, axis)


WIDE = False


def mx_kscale(k):
    if not WIDE:
        return np.ones(k)
    levels = np.array([10, -10, 5, -5, 0])
    if k % 512:
        return np.exp2(np.random.permutation(np.resize(levels, k // 32))).repeat(32)
    a = np.empty((k // 512, 16))
    for p in range(k // 512):
        a[p, :8] = np.random.permutation(np.resize(levels, 8))
        for g in range(8):
            far = levels[np.abs(levels - a[p, g]) >= 10]
            a[p, g + 8] = far[np.random.randint(len(far))]
    return np.exp2(a.ravel()).repeat(32)


BF16 = ml_dtypes.bfloat16


def bf(x):
    return np.asarray(x, np.float32).astype(BF16)


def f64(x):
    return np.asarray(x).astype(np.float64)


B, S, D, QC, KVC, FF = 1, 512, 1024, 8, 2, 4096
EPS = 1e-5


def rmsnorm(u, w):
    return u / np.sqrt(np.square(u).mean(-1, keepdims=True) + EPS) * w


def setup_inputs():
    s = mx_kscale(D)
    t = np.exp2(np.round(np.log2(mx_kscale(FF)) / 2))
    return {"h_attn": bf(np.random.standard_normal((B, S, D)) * 1.3),
            "norm2_w": bf((1.0 + 0.1 * np.random.standard_normal(D)) * s),
            "ffn_wk": bf(np.random.standard_normal((D, FF)) / np.sqrt(D) / s[:, None] * t),
            "ffn_wv": bf(np.random.standard_normal((FF, D)) / np.sqrt(FF) / (t * t)[:, None])}


def reference(h_attn, norm2_w, ffn_wk, ffn_wv):
    h = f64(h_attn)
    hn = rmsnorm(h, f64(norm2_w))
    k = np.square(np.maximum(mxq(hn, 2, "e4m3") @ mxq(f64(ffn_wk), 0, "e4m3"), 0.0))
    return h + (mxq(k, 2, "e4m3") @ mxq(f64(ffn_wv), 0, "e4m3"))

@@ -1,0 +1,215 @@
+from contextlib import ExitStack
+
+import concourse.mybir as mybir
+from concourse.masks import make_identity
+
+F32 = mybir.dt.float32
+BF16 = mybir.dt.bfloat16
+U32 = mybir.dt.uint32
+U8 = mybir.dt.uint8
+FP8X4 = mybir.dt.float8_e4m3fn_x4
+ACT = mybir.ActivationFunctionType
+ALU = mybir.AluOpType
+
+P = 128
+PACK = 4
+K_PASS = P * PACK
+
+TOKENS = 512
+D_MODEL = 1024
+D_FF = 4096
+EPS = 1e-5
+
+TOK_TILES = TOKENS // P
+D_PASSES = D_MODEL // K_PASS
+FF_GROUPS = D_FF // K_PASS
+BANK = 512
+OUT_HALVES = D_MODEL // BANK
+RUN = 4
+PIECE = 256
+
+FLOPS = 2 * 2 * TOKENS * D_MODEL * D_FF
+
+
+def regroup_units(copy, grouped, rows):
+    copy(
+        out=grouped.rearrange("p t m j -> p m j t"),
+        in_=rows.rearrange("p j (m t) -> p m j t", t=PACK),
+    )
+
+
+def regroup(copy, grouped, rows):
+    copy(
+        out=grouped.rearrange("p (c i) t -> p c t i", i=RUN),
+        in_=rows.rearrange("p t (c i) -> p c t i", i=RUN),
+    )
+
+
+def tile_block_pc_kernel(tc, h_attn, norm2_w, ffn_wk, ffn_wv, out):
+    nc = tc.nc
+    h_rows = h_attn.flatten_outer_dims().rearrange("(n p) d -> n p d", p=P)
+    out_rows = out.flatten_outer_dims().rearrange("(n p) d -> n p d", p=P)
+    wk_rows = ffn_wk.rearrange("(c p t) f -> c p t f", t=PACK, p=P)
+    wv_rows = ffn_wv.rearrange("(g p t) d -> g p t d", t=PACK, p=P)
+
+    with ExitStack() as ctx:
+        keep = ctx.enter_context(tc.tile_pool(name="keep", bufs=1))
+        wk_loads = ctx.enter_context(tc.tile_pool(name="wk_loads", bufs=4))
+        wv_loads = ctx.enter_context(tc.tile_pool(name="wv_loads", bufs=FF_GROUPS))
+        grouped = ctx.enter_context(tc.tile_pool(name="grouped", bufs=3))
+        wk_quantised = ctx.enter_context(tc.tile_pool(name="wk_quantised", bufs=3))
+        wv_quantised = ctx.enter_context(tc.tile_pool(name="wv_quantised", bufs=FF_GROUPS))
+        work = ctx.enter_context(tc.tile_pool(name="work", bufs=2))
+        results = ctx.enter_context(tc.tile_pool(name="results", bufs=4))
+        psum = ctx.enter_context(tc.psum_pool(name="psum", bufs=4))
+
+        gain_row = keep.tile([P, D_MODEL], BF16)
+        nc.vector.memset(gain_row[:], 0.0)
+        nc.sync.dma_start(out=gain_row[0:1, :], in_=norm2_w.rearrange("(o d) -> o d", o=1))
+        h_sb = keep.tile([P, TOK_TILES, D_MODEL], BF16)
+        for n in range(TOK_TILES):
+            nc.sync.dma_start(out=h_sb[:, n, :], in_=h_rows[n])
+
+        identity = keep.tile([P, P], BF16)
+        make_identity(nc, identity[:])
+        ones = keep.tile([P, P], BF16)
+        nc.vector.memset(ones[:], 1.0)
+        eps = keep.tile([P, 1], F32)
+        nc.vector.memset(eps[:], EPS)
+        table_warm = keep.tile([P, 1], F32)
+        nc.scalar.activation(out=table_warm[:], in_=eps[:], func=ACT.Sqrt)
+
+        gain = keep.tile([P, PACK, D_MODEL // PACK], F32)
+        for half in range(D_MODEL // BANK):
+            cols = slice(half * BANK, (half + 1) * BANK)
+            gain_ps = psum.tile([P, BANK], F32, tag="bank")
+            nc.tensor.matmul(out=gain_ps[:], lhsT=ones[:], rhs=gain_row[:, cols], start=True, stop=True)
+            cms = slice(half * P, (half + 1) * P)
+            nc.vector.tensor_copy(out=gain[:, :, cms], in_=gain_ps[:].rearrange("p (m t) -> p t m", t=PACK))
+
+        sum_sq = keep.tile([P, TOK_TILES], F32)
+        rms = keep.tile([P, TOK_TILES], F32)
+        inv_rms = keep.tile([P, TOK_TILES], F32)
+        hn_grouped = keep.tile([P, TOK_TILES, D_PASSES, P, PACK], BF16, align_bytes=64)
+        hn_codes = keep.tile([P, TOK_TILES, D_PASSES, P], U32, align_bytes=64)
+        hn_scales = keep.tile([P, TOK_TILES, D_PASSES, P], U8, align_bytes=64)
+        for n in range(TOK_TILES):
+            one = slice(n, n + 1)
+            squares = work.tile([P, D_MODEL], BF16)
+            nc.scalar.activation(out=squares[:], in_=h_sb[:, n, :], func=ACT.Square, accum_out=sum_sq[:, one])
+            nc.scalar.activation(
+                out=rms[:, one], in_=sum_sq[:, one], func=ACT.Sqrt, bias=eps[:], scale=1.0 / D_MODEL
+            )
+            nc.vector.reciprocal(out=inv_rms[:, one], in_=rms[:, one])
+            hn = work.tile([P, PACK, D_MODEL // PACK], BF16)
+            nc.vector.scalar_tensor_tensor(
+                out=hn[:],
+                in0=h_sb[:, n, :].rearrange("p (cm t) -> p t cm", t=PACK),
+                scalar=inv_rms[:, one],
+                in1=gain[:],
+                op0=ALU.mult,
+                op1=ALU.mult,
+            )
+            hn_t = psum.tile([P, D_PASSES, PACK, P], BF16, tag="bank")
+            for c in range(D_PASSES):
+                for t in range(PACK):
+                    nc.tensor.transpose(hn_t[:, c, t, :], hn[:, t, c * P : (c + 1) * P], identity[:])
+            nc.scalar.copy(out=hn_grouped[:, n], in_=hn_t[:].rearrange("p c t k -> p c k t"))
+            nc.vector.quantize_mx(
+                out=hn_codes[:, n].rearrange("p c k -> p (c k)").bitcast(FP8X4),
+                scales=hn_scales[:, n].rearrange("p c k -> p (c k)"),
+                in_=hn_grouped[:, n].rearrange("p c k t -> p (c k t)"),
+            )
+
+        k_codes = keep.tile([P, FF_GROUPS, TOKENS], U32, align_bytes=64)
+        k_scales = keep.tile([P, FF_GROUPS, TOKENS], U8, align_bytes=64)
+
+        def hidden_group(g):
+            wk_raw = wk_loads.tile([P, D_PASSES * PACK, K_PASS], BF16)
+            for c in range(D_PASSES):
+                nc.sync.dma_start(
+                    out=wk_raw[:, c * PACK : (c + 1) * PACK, :], in_=wk_rows[c, :, :, g * K_PASS : (g + 1) * K_PASS]
+                )
+            wk_grouped = grouped.tile([P, D_PASSES, PACK, P, PACK], BF16, align_bytes=64)
+            for c in range(D_PASSES):
+                for first in range(0, K_PASS, PIECE):
+                    cols = slice(first, first + PIECE)
+                    ms = slice(first // PACK, (first + PIECE) // PACK)
+                    regroup_units(
+                        nc.any.tensor_copy, wk_grouped[:, c, :, ms, :], wk_raw[:, c * PACK : (c + 1) * PACK, cols]
+                    )
+            wk_codes = wk_quantised.tile([P, D_PASSES, K_PASS], U32, align_bytes=64)
+            wk_scales = wk_quantised.tile([P, D_PASSES, K_PASS], U8, align_bytes=64)
+            nc.vector.quantize_mx(
+                out=wk_codes[:].rearrange("p c f -> p (c f)").bitcast(FP8X4),
+                scales=wk_scales[:].rearrange("p c f -> p (c f)"),
+                in_=wk_grouped[:].rearrange("p c t m j -> p (c t m j)"),
+            )
+            relu = work.tile([P, TOKENS, PACK], F32)
+            for n in range(TOK_TILES):
+                toks = slice(n * P, (n + 1) * P)
+                pre = psum.tile([P, PACK, P], F32, tag="bank")
+                for t in range(PACK):
+                    units = slice(t * P, (t + 1) * P)
+                    for c in range(D_PASSES):
+                        nc.tensor.matmul_mx(
+                            out=pre[:, t, :],
+                            lhsT=wk_codes[:, c, units].bitcast(FP8X4),
+                            lhsT_scale=wk_scales[:, c, units],
+                            rhs=hn_codes[:, n, c, :].bitcast(FP8X4),
+                            rhs_scale=hn_scales[:, n, c, :],
+                            start=(c == 0),
+                            stop=(c == D_PASSES - 1),
+                        )
+                nc.scalar.activation(out=relu[:, toks, :], in_=pre[:].rearrange("p t k -> p k t"), func=ACT.Relu)
+            k_grouped = grouped.tile([P, TOKENS, PACK], BF16, align_bytes=64)
+            nc.scalar.activation(out=k_grouped[:], in_=relu[:], func=ACT.Square)
+            nc.vector.quantize_mx(
+                out=k_codes[:, g, :].bitcast(FP8X4),
+                scales=k_scales[:, g, :],
+                in_=k_grouped[:].rearrange("p k t -> p (k t)"),
+            )
+
+        def add_group_to_sums(g, half, sums):
+            wv_raw = wv_loads.tile([P, PACK, BANK], BF16)
+            nc.sync.dma_start(out=wv_raw[:], in_=wv_rows[g, :, :, half * BANK : (half + 1) * BANK])
+            wv_grouped = grouped.tile([P, BANK, PACK], BF16, align_bytes=64)
+            for first in range(0, BANK, PIECE):
+                cols = slice(first, first + PIECE)
+                regroup(nc.any.tensor_copy, wv_grouped[:, cols, :], wv_raw[:, :, cols])
+            wv_codes = wv_quantised.tile([P, BANK], U32, align_bytes=64)
+            wv_scales = wv_quantised.tile([P, BANK], U8, align_bytes=64)
+            nc.vector.quantize_mx(
+                out=wv_codes[:].bitcast(FP8X4),
+                scales=wv_scales[:],
+                in_=wv_grouped[:].rearrange("p d t -> p (d t)"),
+            )
+            for n in range(TOK_TILES):
+                toks = slice(n * P, (n + 1) * P)
+                nc.tensor.matmul_mx(
+                    out=sums[n][:],
+                    lhsT=k_codes[:, g, toks].bitcast(FP8X4),
+                    lhsT_scale=k_scales[:, g, toks],
+                    rhs=wv_codes[:].bitcast(FP8X4),
+                    rhs_scale=wv_scales[:],
+                    start=(g == 0),
+                    stop=(g == FF_GROUPS - 1),
+                )
+
+        def add_residual_and_store(half, sums):
+            cols = slice(half * BANK, (half + 1) * BANK)
+            for n in range(TOK_TILES):
+                result = results.tile([P, BANK], F32)
+                nc.vector.tensor_tensor(out=result[:], in0=sums[n][:], in1=h_sb[:, n, cols], op=ALU.add)
+                nc.sync.dma_start(out=out_rows[n][:, cols], in_=result[:])
+
+        sums = [psum.tile([P, BANK], F32, tag="sums", name="sums%d" % n) for n in range(TOK_TILES)]
+        for g in range(FF_GROUPS):
+            hidden_group(g)
+            add_group_to_sums(g, 0, sums)
+        add_residual_and_store(0, sums)
+
+        sums = [psum.tile([P, BANK], F32, tag="bank", name="sums%d" % n) for n in range(TOK_TILES)]
+        for g in range(FF_GROUPS):
+            add_group_to_sums(g, 1, sums)
+        add_residual_and_store(1, sums)

@@ -24,24 +24,24 @@ TOK_TILES = TOKENS // P
 D_PASSES = D_MODEL // K_PASS
 FF_GROUPS = D_FF // K_PASS
 BANK = 512
-OUT_HALVES = D_MODEL // BANK
-RUN = 4
 PIECE = 256
+RUN = 4
+EARLY = 6
 
 FLOPS = 2 * 2 * TOKENS * D_MODEL * D_FF
-
-
-def regroup_units(copy, grouped, rows):
-    copy(
-        out=grouped.rearrange("p t m j -> p m j t"),
-        in_=rows.rearrange("p j (m t) -> p m j t", t=PACK),
-    )
 
 
 def regroup(copy, grouped, rows):
     copy(
         out=grouped.rearrange("p (c i) t -> p c t i", i=RUN),
         in_=rows.rearrange("p t (c i) -> p c t i", i=RUN),
+    )
+
+
+def regroup_units(copy, grouped, rows):
+    copy(
+        out=grouped.rearrange("p t m j -> p m j t"),
+        in_=rows.rearrange("p j (m t) -> p m j t", t=PACK),
     )
 
 
@@ -54,24 +54,48 @@ def tile_block_pc_kernel(tc, h_attn, norm2_w, ffn_wk, ffn_wv, out):
 
     with ExitStack() as ctx:
         keep = ctx.enter_context(tc.tile_pool(name="keep", bufs=1))
-        wk_loads = ctx.enter_context(tc.tile_pool(name="wk_loads", bufs=4))
-        wv_loads = ctx.enter_context(tc.tile_pool(name="wv_loads", bufs=FF_GROUPS))
-        grouped = ctx.enter_context(tc.tile_pool(name="grouped", bufs=3))
-        wk_quantised = ctx.enter_context(tc.tile_pool(name="wk_quantised", bufs=3))
-        wv_quantised = ctx.enter_context(tc.tile_pool(name="wv_quantised", bufs=FF_GROUPS))
+        wk_loads = ctx.enter_context(tc.tile_pool(name="wk_loads", bufs=3))
+        grouped = ctx.enter_context(tc.tile_pool(name="grouped", bufs=2))
+        quantised = ctx.enter_context(tc.tile_pool(name="quantised", bufs=2))
         work = ctx.enter_context(tc.tile_pool(name="work", bufs=2))
-        results = ctx.enter_context(tc.tile_pool(name="results", bufs=4))
-        psum = ctx.enter_context(tc.psum_pool(name="psum", bufs=4))
+        results = ctx.enter_context(tc.tile_pool(name="results", bufs=8))
+        psum = ctx.enter_context(tc.psum_pool(name="psum", bufs=3))
+        ctx.enter_context(tc.manual_schedule())
 
-        gain_row = keep.tile([P, D_MODEL], BF16)
-        nc.vector.memset(gain_row[:], 0.0)
-        nc.sync.dma_start(out=gain_row[0:1, :], in_=norm2_w.rearrange("(o d) -> o d", o=1))
         h_sb = keep.tile([P, TOK_TILES, D_MODEL], BF16)
-        for n in range(TOK_TILES):
+        wv_raw = keep.tile([P, FF_GROUPS, PACK, D_MODEL], BF16)
+        gain_row = keep.tile([P, D_MODEL], BF16)
+        nc.vector.memset(gain_row[:].bitcast(U32), 0)
+        wk_raws = {}
+
+        def load_h(n):
             nc.sync.dma_start(out=h_sb[:, n, :], in_=h_rows[n])
 
-        identity = keep.tile([P, P], BF16)
+        def load_wk(g, c):
+            if c == 0:
+                wk_raws[g] = wk_loads.tile([P, D_PASSES, PACK, K_PASS], BF16, name="wk_raw")
+            nc.sync.dma_start(out=wk_raws[g][:, c], in_=wk_rows[c, :, :, g * K_PASS : (g + 1) * K_PASS])
+
+        def load_wv(g):
+            nc.sync.dma_start(out=wv_raw[:, g], in_=wv_rows[g])
+
+        load_h(0)
+        load_wk(0, 0)
+        nc.sync.dma_start(out=gain_row[0:1, :], in_=norm2_w.rearrange("(o d) -> o d", o=1))
+        load_h(1)
+        load_wk(0, 1)
+        load_h(2)
+        load_h(3)
+        load_wv(0)
+        for g in range(1, 3):
+            for c in range(D_PASSES):
+                load_wk(g, c)
+            load_wv(g)
+
+        identity = keep.tile([P, P], F32)
         make_identity(nc, identity[:])
+        identity_bf16 = keep.tile([P, P], BF16)
+        nc.gpsimd.tensor_copy(out=identity_bf16[:], in_=identity[:])
         ones = keep.tile([P, P], BF16)
         nc.vector.memset(ones[:], 1.0)
         eps = keep.tile([P, 1], F32)
@@ -79,137 +103,306 @@ def tile_block_pc_kernel(tc, h_attn, norm2_w, ffn_wk, ffn_wv, out):
         table_warm = keep.tile([P, 1], F32)
         nc.scalar.activation(out=table_warm[:], in_=eps[:], func=ACT.Sqrt)
 
-        gain = keep.tile([P, PACK, D_MODEL // PACK], F32)
-        for half in range(D_MODEL // BANK):
-            cols = slice(half * BANK, (half + 1) * BANK)
-            gain_ps = psum.tile([P, BANK], F32, tag="bank")
-            nc.tensor.matmul(out=gain_ps[:], lhsT=ones[:], rhs=gain_row[:, cols], start=True, stop=True)
-            cms = slice(half * P, (half + 1) * P)
-            nc.vector.tensor_copy(out=gain[:, :, cms], in_=gain_ps[:].rearrange("p (m t) -> p t m", t=PACK))
-
+        gain = keep.tile([P, D_MODEL], BF16)
         sum_sq = keep.tile([P, TOK_TILES], F32)
         rms = keep.tile([P, TOK_TILES], F32)
         inv_rms = keep.tile([P, TOK_TILES], F32)
-        hn_grouped = keep.tile([P, TOK_TILES, D_PASSES, P, PACK], BF16, align_bytes=64)
         hn_codes = keep.tile([P, TOK_TILES, D_PASSES, P], U32, align_bytes=64)
         hn_scales = keep.tile([P, TOK_TILES, D_PASSES, P], U8, align_bytes=64)
-        for n in range(TOK_TILES):
+        hn_tiles = {}
+        hn_banks = {}
+
+        def spread_gain():
+            gain_ps = psum.tile([P, D_MODEL], BF16, tag="bank", name="gain_ps")
+            for first in range(0, D_MODEL, BANK):
+                cols = slice(first, first + BANK)
+                nc.tensor.matmul(out=gain_ps[:, cols], lhsT=ones[:], rhs=gain_row[:, cols], start=True, stop=True)
+            nc.vector.tensor_copy(out=gain[:], in_=gain_ps[:])
+
+        def measure(n):
             one = slice(n, n + 1)
-            squares = work.tile([P, D_MODEL], BF16)
+            squares = work.tile([P, D_MODEL], BF16, name="squares")
             nc.scalar.activation(out=squares[:], in_=h_sb[:, n, :], func=ACT.Square, accum_out=sum_sq[:, one])
             nc.scalar.activation(
                 out=rms[:, one], in_=sum_sq[:, one], func=ACT.Sqrt, bias=eps[:], scale=1.0 / D_MODEL
             )
+
+        def normalise(n):
+            one = slice(n, n + 1)
             nc.vector.reciprocal(out=inv_rms[:, one], in_=rms[:, one])
-            hn = work.tile([P, PACK, D_MODEL // PACK], BF16)
+            hn_tiles[n] = work.tile([P, D_MODEL], BF16, name="hn")
             nc.vector.scalar_tensor_tensor(
-                out=hn[:],
-                in0=h_sb[:, n, :].rearrange("p (cm t) -> p t cm", t=PACK),
+                out=hn_tiles[n][:],
+                in0=h_sb[:, n, :],
                 scalar=inv_rms[:, one],
                 in1=gain[:],
                 op0=ALU.mult,
                 op1=ALU.mult,
             )
-            hn_t = psum.tile([P, D_PASSES, PACK, P], BF16, tag="bank")
+
+        def turn(n):
+            words = hn_tiles[n][:].bitcast(F32)
+            hn_banks[n] = psum.tile([P, D_PASSES, 2, P], F32, tag="bank", name="hn_bank")
             for c in range(D_PASSES):
-                for t in range(PACK):
-                    nc.tensor.transpose(hn_t[:, c, t, :], hn[:, t, c * P : (c + 1) * P], identity[:])
-            nc.scalar.copy(out=hn_grouped[:, n], in_=hn_t[:].rearrange("p c t k -> p c k t"))
+                for u in range(2):
+                    pairs = slice(c * 2 * P + u, (c + 1) * 2 * P, 2)
+                    nc.tensor.transpose(hn_banks[n][:, c, u, :], words[:, pairs], identity[:])
+
+        def group_hn(n):
+            hn_tiles[n] = work.tile([P, D_PASSES, P, PACK], BF16, align_bytes=64, name="hn_grouped")
+            nc.scalar.copy(
+                out=hn_tiles[n][:].rearrange("p c k t -> p (c k t)").bitcast(F32).rearrange("p (c k u) -> p c k u", c=D_PASSES, u=2),
+                in_=hn_banks[n][:].rearrange("p c u k -> p c k u"),
+            )
+
+        def quantise_hn(n):
             nc.vector.quantize_mx(
                 out=hn_codes[:, n].rearrange("p c k -> p (c k)").bitcast(FP8X4),
                 scales=hn_scales[:, n].rearrange("p c k -> p (c k)"),
-                in_=hn_grouped[:, n].rearrange("p c k t -> p (c k t)"),
+                in_=hn_tiles[n][:].rearrange("p c k t -> p (c k t)"),
             )
+
+        wk_grouped = {}
+        wk_quantised = {}
+
+        def group_wk(g, c):
+            if c == 0:
+                wk_grouped[g] = grouped.tile([P, D_PASSES, PACK, P, PACK], BF16, align_bytes=64, name="wk_grouped")
+            regroup_units(nc.vector.tensor_copy, wk_grouped[g][:, c], wk_raws[g][:, c])
+
+        def quantise_wk(g):
+            codes = quantised.tile([P, D_PASSES, K_PASS], U32, align_bytes=64, name="wk_codes")
+            scales = quantised.tile([P, D_PASSES, K_PASS], U8, align_bytes=64, name="wk_scales")
+            nc.vector.quantize_mx(
+                out=codes[:].rearrange("p c f -> p (c f)").bitcast(FP8X4),
+                scales=scales[:].rearrange("p c f -> p (c f)"),
+                in_=wk_grouped[g][:].rearrange("p c t m j -> p (c t m j)"),
+            )
+            wk_quantised[g] = codes, scales
+
+        wv_grouped = {}
+        wv_quantised = {}
+        stages = {}
+
+        def grouped_wv(g, quarter):
+            if quarter < 2:
+                if (g, 0) not in wv_grouped:
+                    wv_grouped[g, 0] = grouped.tile([P, BANK, PACK], BF16, align_bytes=64, name="wv_half")
+                return wv_grouped[g, 0][:, quarter * PIECE : (quarter + 1) * PIECE, :]
+            if (g, quarter) not in wv_grouped:
+                wv_grouped[g, quarter] = grouped.tile([P, PIECE, PACK], BF16, align_bytes=64, bufs=4, name="wv_quarter")
+            return wv_grouped[g, quarter][:]
+
+        def group_wv(g, quarter, copy):
+            regroup(copy, grouped_wv(g, quarter), wv_raw[:, g, :, quarter * PIECE : (quarter + 1) * PIECE])
+
+        def stage_wv(g, quarter):
+            stages[g, quarter] = psum.tile([P, PIECE, PACK], BF16, tag="stage", bufs=1, name="stage")
+            for first in range(0, PIECE, P):
+                cols = slice(quarter * PIECE + first, quarter * PIECE + first + P)
+                nc.tensor.matmul(
+                    out=stages[g, quarter][:, first : first + P, :].rearrange("p (b i) t -> p b t i", i=8),
+                    lhsT=identity_bf16[:],
+                    rhs=wv_raw[:, g, :, cols].rearrange("p t (b i) -> p b t i", i=8),
+                    start=True,
+                    stop=True,
+                )
+
+        def unstage_wv(g, quarter):
+            nc.scalar.copy(out=grouped_wv(g, quarter), in_=stages[g, quarter][:])
+
+        def quantise_wv(g, quarter):
+            width = BANK if quarter < 2 else PIECE
+            bufs = {2: FF_GROUPS, 3: 6}.get(quarter, 2)
+            kind = ("half", "half", "third", "fourth")[quarter]
+            codes = quantised.tile([P, width], U32, align_bytes=64, bufs=bufs, name="wv_codes_" + kind)
+            scales = quantised.tile([P, width], U8, align_bytes=64, bufs=bufs, name="wv_scales_" + kind)
+            nc.vector.quantize_mx(
+                out=codes[:].bitcast(FP8X4),
+                scales=scales[:],
+                in_=wv_grouped[g, quarter][:].rearrange("p d t -> p (d t)"),
+            )
+            wv_quantised[g, quarter] = codes, scales
 
         k_codes = keep.tile([P, FF_GROUPS, TOKENS], U32, align_bytes=64)
         k_scales = keep.tile([P, FF_GROUPS, TOKENS], U8, align_bytes=64)
+        pre_banks = {}
+        relus = {}
+        k_grouped = {}
 
-        def hidden_group(g):
-            wk_raw = wk_loads.tile([P, D_PASSES * PACK, K_PASS], BF16)
-            for c in range(D_PASSES):
-                nc.sync.dma_start(
-                    out=wk_raw[:, c * PACK : (c + 1) * PACK, :], in_=wk_rows[c, :, :, g * K_PASS : (g + 1) * K_PASS]
-                )
-            wk_grouped = grouped.tile([P, D_PASSES, PACK, P, PACK], BF16, align_bytes=64)
-            for c in range(D_PASSES):
-                for first in range(0, K_PASS, PIECE):
-                    cols = slice(first, first + PIECE)
-                    ms = slice(first // PACK, (first + PIECE) // PACK)
-                    regroup_units(
-                        nc.any.tensor_copy, wk_grouped[:, c, :, ms, :], wk_raw[:, c * PACK : (c + 1) * PACK, cols]
+        def multiply_hidden(g, n):
+            pre = psum.tile([P, PACK, P], F32, tag="bank", name="pre")
+            codes, scales = wk_quantised[g]
+            for t in range(PACK):
+                units = slice(t * P, (t + 1) * P)
+                for c in range(D_PASSES):
+                    nc.tensor.matmul_mx(
+                        out=pre[:, t, :],
+                        lhsT=codes[:, c, units].bitcast(FP8X4),
+                        lhsT_scale=scales[:, c, units],
+                        rhs=hn_codes[:, n, c, :].bitcast(FP8X4),
+                        rhs_scale=hn_scales[:, n, c, :],
+                        start=(c == 0),
+                        stop=(c == D_PASSES - 1),
                     )
-            wk_codes = wk_quantised.tile([P, D_PASSES, K_PASS], U32, align_bytes=64)
-            wk_scales = wk_quantised.tile([P, D_PASSES, K_PASS], U8, align_bytes=64)
-            nc.vector.quantize_mx(
-                out=wk_codes[:].rearrange("p c f -> p (c f)").bitcast(FP8X4),
-                scales=wk_scales[:].rearrange("p c f -> p (c f)"),
-                in_=wk_grouped[:].rearrange("p c t m j -> p (c t m j)"),
+            pre_banks[g, n] = pre
+
+        def rectify(g, n):
+            if n == 0:
+                relus[g] = work.tile([P, TOKENS, PACK], F32, bufs=1, name="relu")
+            nc.scalar.activation(
+                out=relus[g][:, n * P : (n + 1) * P, :],
+                in_=pre_banks[g, n][:].rearrange("p t k -> p k t"),
+                func=ACT.Relu,
             )
-            relu = work.tile([P, TOKENS, PACK], F32)
-            for n in range(TOK_TILES):
-                toks = slice(n * P, (n + 1) * P)
-                pre = psum.tile([P, PACK, P], F32, tag="bank")
-                for t in range(PACK):
-                    units = slice(t * P, (t + 1) * P)
-                    for c in range(D_PASSES):
-                        nc.tensor.matmul_mx(
-                            out=pre[:, t, :],
-                            lhsT=wk_codes[:, c, units].bitcast(FP8X4),
-                            lhsT_scale=wk_scales[:, c, units],
-                            rhs=hn_codes[:, n, c, :].bitcast(FP8X4),
-                            rhs_scale=hn_scales[:, n, c, :],
-                            start=(c == 0),
-                            stop=(c == D_PASSES - 1),
-                        )
-                nc.scalar.activation(out=relu[:, toks, :], in_=pre[:].rearrange("p t k -> p k t"), func=ACT.Relu)
-            k_grouped = grouped.tile([P, TOKENS, PACK], BF16, align_bytes=64)
-            nc.scalar.activation(out=k_grouped[:], in_=relu[:], func=ACT.Square)
+
+        def square(g):
+            k_grouped[g] = grouped.tile([P, TOKENS, PACK], BF16, align_bytes=64, name="k_grouped")
+            nc.scalar.activation(out=k_grouped[g][:], in_=relus[g][:], func=ACT.Square)
+
+        def quantise_k(g):
             nc.vector.quantize_mx(
                 out=k_codes[:, g, :].bitcast(FP8X4),
                 scales=k_scales[:, g, :],
-                in_=k_grouped[:].rearrange("p k t -> p (k t)"),
+                in_=k_grouped[g][:].rearrange("p k t -> p (k t)"),
             )
 
-        def add_group_to_sums(g, half, sums):
-            wv_raw = wv_loads.tile([P, PACK, BANK], BF16)
-            nc.sync.dma_start(out=wv_raw[:], in_=wv_rows[g, :, :, half * BANK : (half + 1) * BANK])
-            wv_grouped = grouped.tile([P, BANK, PACK], BF16, align_bytes=64)
-            for first in range(0, BANK, PIECE):
-                cols = slice(first, first + PIECE)
-                regroup(nc.any.tensor_copy, wv_grouped[:, cols, :], wv_raw[:, :, cols])
-            wv_codes = wv_quantised.tile([P, BANK], U32, align_bytes=64)
-            wv_scales = wv_quantised.tile([P, BANK], U8, align_bytes=64)
-            nc.vector.quantize_mx(
-                out=wv_codes[:].bitcast(FP8X4),
-                scales=wv_scales[:],
-                in_=wv_grouped[:].rearrange("p d t -> p (d t)"),
-            )
+        def open_sums(tags, width):
+            bufs = {"sums": 4, "bank": 3, "stage": 1}
+            return [
+                psum.tile([P, width], F32, tag=tag, bufs=bufs[tag], name="sums%d" % n) for n, tag in enumerate(tags)
+            ]
+
+        def add_to_sums(g, quarter, sums):
+            codes, scales = wv_quantised[g, quarter]
             for n in range(TOK_TILES):
                 toks = slice(n * P, (n + 1) * P)
                 nc.tensor.matmul_mx(
                     out=sums[n][:],
                     lhsT=k_codes[:, g, toks].bitcast(FP8X4),
                     lhsT_scale=k_scales[:, g, toks],
-                    rhs=wv_codes[:].bitcast(FP8X4),
-                    rhs_scale=wv_scales[:],
+                    rhs=codes[:].bitcast(FP8X4),
+                    rhs_scale=scales[:],
                     start=(g == 0),
                     stop=(g == FF_GROUPS - 1),
                 )
 
-        def add_residual_and_store(half, sums):
-            cols = slice(half * BANK, (half + 1) * BANK)
+        def add_residual_and_store(quarter, sums):
+            width = sums[0].shape[1]
+            cols = slice(quarter * PIECE, quarter * PIECE + width)
             for n in range(TOK_TILES):
-                result = results.tile([P, BANK], F32)
-                nc.vector.tensor_tensor(out=result[:], in0=sums[n][:], in1=h_sb[:, n, cols], op=ALU.add)
-                nc.sync.dma_start(out=out_rows[n][:, cols], in_=result[:])
+                result = results.tile([P, BANK], F32, name="result")
+                nc.vector.tensor_tensor(
+                    out=result[:, :width], in0=sums[n][:], in1=h_sb[:, n, cols], op=ALU.add
+                )
+                nc.sync.dma_start(out=out_rows[n][:, cols], in_=result[:, :width])
 
-        sums = [psum.tile([P, BANK], F32, tag="sums", name="sums%d" % n) for n in range(TOK_TILES)]
-        for g in range(FF_GROUPS):
-            hidden_group(g)
-            add_group_to_sums(g, 0, sums)
-        add_residual_and_store(0, sums)
+        on_scalar = nc.scalar.copy
+        on_vector = nc.vector.tensor_copy
+        measure(0)
+        group_wk(0, 0)
+        spread_gain()
+        measure(1)
+        normalise(0)
+        turn(0)
+        group_wk(0, 1)
+        measure(2)
+        group_hn(0)
+        normalise(1)
+        turn(1)
+        measure(3)
+        group_hn(1)
+        stage_wv(0, 0)
+        unstage_wv(0, 0)
+        quantise_hn(0)
+        quantise_wk(0)
+        multiply_hidden(0, 0)
+        group_wv(0, 3, on_scalar)
+        normalise(2)
+        turn(2)
+        quantise_hn(1)
+        multiply_hidden(0, 1)
+        group_hn(2)
+        rectify(0, 0)
+        normalise(3)
+        turn(3)
+        rectify(0, 1)
+        quantise_hn(2)
+        multiply_hidden(0, 2)
+        group_hn(3)
+        rectify(0, 2)
+        group_wk(1, 0)
+        stage_wv(0, 1)
+        unstage_wv(0, 1)
+        quantise_hn(3)
+        multiply_hidden(0, 3)
+        rectify(0, 3)
+        quantise_wv(0, 3)
 
-        sums = [psum.tile([P, BANK], F32, tag="bank", name="sums%d" % n) for n in range(TOK_TILES)]
+        first_half = open_sums(["sums"] * 4, BANK)
         for g in range(FF_GROUPS):
-            add_group_to_sums(g, 1, sums)
-        add_residual_and_store(1, sums)
+            more = g + 1 < FF_GROUPS
+            if g > 0:
+                for n in range(TOK_TILES):
+                    multiply_hidden(g, n)
+                    rectify(g, n)
+                    if n == 1:
+                        stage_wv(g, 1)
+                        unstage_wv(g, 1)
+            square(g)
+            if more and g > 0:
+                group_wk(g + 1, 0)
+            elif g > 0:
+                for j in range(1, 3):
+                    group_wv(j, 3, on_vector)
+                    quantise_wv(j, 3)
+            if g > 0:
+                quantise_k(g - 1)
+                add_to_sums(g - 1, 0, first_half)
+            if more:
+                stage_wv(g + 1, 0)
+                unstage_wv(g + 1, 0)
+            if more:
+                group_wk(g + 1, 1)
+            else:
+                for j in range(3, 5):
+                    group_wv(j, 3, on_vector)
+                    quantise_wv(j, 3)
+            quantise_wv(g, 0)
+            if g < EARLY:
+                group_wv(g, 2, on_vector)
+            if more:
+                quantise_wk(g + 1)
+            if g < EARLY:
+                quantise_wv(g, 2)
+            if g + 3 < FF_GROUPS:
+                for c in range(D_PASSES):
+                    load_wk(g + 3, c)
+                load_wv(g + 3)
+
+        last = FF_GROUPS - 1
+        third = open_sums(["bank"] * 3 + ["stage"], PIECE)
+        for g in range(FF_GROUPS):
+            if not (g < EARLY):
+                group_wv(g, 2, on_vector)
+        for g in range(FF_GROUPS - 1):
+            if not (g < EARLY):
+                quantise_wv(g, 2)
+            if g == 4:
+                quantise_k(last)
+                add_to_sums(last, 0, first_half)
+            add_to_sums(g, 2, third)
+        if not (last < EARLY):
+            quantise_wv(last, 2)
+        add_to_sums(last, 2, third)
+        add_residual_and_store(0, first_half)
+        fourth = open_sums(["sums"] * 4, PIECE)
+        for g in range(FF_GROUPS):
+            if (g, 3) not in wv_grouped:
+                group_wv(g, 3, on_scalar)
+            if (g, 3) not in wv_quantised:
+                quantise_wv(g, 3)
+            add_to_sums(g, 3, fourth)
+            if g == 5:
+                add_residual_and_store(2, third)
+        add_residual_and_store(3, fourth)

@@ -26,7 +26,6 @@ FF_GROUPS = D_FF // K_PASS
 BANK = 512
 PIECE = 256
 RUN = 4
-EARLY = 6
 
 FLOPS = 2 * 2 * TOKENS * D_MODEL * D_FF
 
@@ -59,7 +58,7 @@ def tile_block_pc_kernel(tc, h_attn, norm2_w, ffn_wk, ffn_wv, out):
         quantised = ctx.enter_context(tc.tile_pool(name="quantised", bufs=2))
         work = ctx.enter_context(tc.tile_pool(name="work", bufs=2))
         results = ctx.enter_context(tc.tile_pool(name="results", bufs=8))
-        psum = ctx.enter_context(tc.psum_pool(name="psum", bufs=3))
+        psum = ctx.enter_context(tc.psum_pool(name="psum", bufs=4))
         ctx.enter_context(tc.manual_schedule())
 
         h_sb = keep.tile([P, TOK_TILES, D_MODEL], BF16)
@@ -94,8 +93,6 @@ def tile_block_pc_kernel(tc, h_attn, norm2_w, ffn_wk, ffn_wv, out):
 
         identity = keep.tile([P, P], F32)
         make_identity(nc, identity[:])
-        identity_bf16 = keep.tile([P, P], BF16)
-        nc.gpsimd.tensor_copy(out=identity_bf16[:], in_=identity[:])
         ones = keep.tile([P, P], BF16)
         nc.vector.memset(ones[:], 1.0)
         eps = keep.tile([P, 1], F32)
@@ -182,7 +179,6 @@ def tile_block_pc_kernel(tc, h_attn, norm2_w, ffn_wk, ffn_wv, out):
 
         wv_grouped = {}
         wv_quantised = {}
-        stages = {}
 
         def grouped_wv(g, quarter):
             if quarter < 2:
@@ -195,21 +191,6 @@ def tile_block_pc_kernel(tc, h_attn, norm2_w, ffn_wk, ffn_wv, out):
 
         def group_wv(g, quarter, copy):
             regroup(copy, grouped_wv(g, quarter), wv_raw[:, g, :, quarter * PIECE : (quarter + 1) * PIECE])
-
-        def stage_wv(g, quarter):
-            stages[g, quarter] = psum.tile([P, PIECE, PACK], BF16, tag="stage", bufs=1, name="stage")
-            for first in range(0, PIECE, P):
-                cols = slice(quarter * PIECE + first, quarter * PIECE + first + P)
-                nc.tensor.matmul(
-                    out=stages[g, quarter][:, first : first + P, :].rearrange("p (b i) t -> p b t i", i=8),
-                    lhsT=identity_bf16[:],
-                    rhs=wv_raw[:, g, :, cols].rearrange("p t (b i) -> p b t i", i=8),
-                    start=True,
-                    stop=True,
-                )
-
-        def unstage_wv(g, quarter):
-            nc.scalar.copy(out=grouped_wv(g, quarter), in_=stages[g, quarter][:])
 
         def quantise_wv(g, quarter):
             width = BANK if quarter < 2 else PIECE
@@ -267,11 +248,8 @@ def tile_block_pc_kernel(tc, h_attn, norm2_w, ffn_wk, ffn_wv, out):
                 in_=k_grouped[g][:].rearrange("p k t -> p (k t)"),
             )
 
-        def open_sums(tags, width):
-            bufs = {"sums": 4, "bank": 3, "stage": 1}
-            return [
-                psum.tile([P, width], F32, tag=tag, bufs=bufs[tag], name="sums%d" % n) for n, tag in enumerate(tags)
-            ]
+        def open_sums(tag, width):
+            return [psum.tile([P, width], F32, tag=tag, name="sums%d" % n) for n in range(TOK_TILES)]
 
         def add_to_sums(g, quarter, sums):
             codes, scales = wv_quantised[g, quarter]
@@ -312,16 +290,15 @@ def tile_block_pc_kernel(tc, h_attn, norm2_w, ffn_wk, ffn_wv, out):
         turn(1)
         measure(3)
         group_hn(1)
-        stage_wv(0, 0)
-        unstage_wv(0, 0)
         quantise_hn(0)
+        group_wv(0, 0, on_scalar)
         quantise_wk(0)
         multiply_hidden(0, 0)
-        group_wv(0, 3, on_scalar)
         normalise(2)
         turn(2)
         quantise_hn(1)
         multiply_hidden(0, 1)
+        group_wv(0, 3, on_scalar)
         group_hn(2)
         rectify(0, 0)
         normalise(3)
@@ -332,48 +309,47 @@ def tile_block_pc_kernel(tc, h_attn, norm2_w, ffn_wk, ffn_wv, out):
         group_hn(3)
         rectify(0, 2)
         group_wk(1, 0)
-        stage_wv(0, 1)
-        unstage_wv(0, 1)
+        group_wv(0, 1, on_vector)
         quantise_hn(3)
         multiply_hidden(0, 3)
         rectify(0, 3)
         quantise_wv(0, 3)
 
-        first_half = open_sums(["sums"] * 4, BANK)
+        first_half = open_sums("sums", BANK)
         for g in range(FF_GROUPS):
             more = g + 1 < FF_GROUPS
             if g > 0:
                 for n in range(TOK_TILES):
                     multiply_hidden(g, n)
                     rectify(g, n)
-                    if n == 1:
-                        stage_wv(g, 1)
-                        unstage_wv(g, 1)
             square(g)
+            if more:
+                group_wv(g + 1, 0, on_scalar)
             if more and g > 0:
                 group_wk(g + 1, 0)
             elif g > 0:
                 for j in range(1, 3):
-                    group_wv(j, 3, on_vector)
-                    quantise_wv(j, 3)
+                    group_wv(j, 2, on_vector)
             if g > 0:
                 quantise_k(g - 1)
                 add_to_sums(g - 1, 0, first_half)
-            if more:
-                stage_wv(g + 1, 0)
-                unstage_wv(g + 1, 0)
+                group_wv(g, 1, on_vector)
             if more:
                 group_wk(g + 1, 1)
             else:
-                for j in range(3, 5):
-                    group_wv(j, 3, on_vector)
-                    quantise_wv(j, 3)
+                for j in range(1, 3):
+                    quantise_wv(j, 2)
+                for j in range(3, 6):
+                    group_wv(j, 2, on_vector)
             quantise_wv(g, 0)
-            if g < EARLY:
+            if not more:
+                for j in range(3, 6):
+                    quantise_wv(j, 2)
+            if g == 0:
                 group_wv(g, 2, on_vector)
             if more:
                 quantise_wk(g + 1)
-            if g < EARLY:
+            if g == 0:
                 quantise_wv(g, 2)
             if g + 3 < FF_GROUPS:
                 for c in range(D_PASSES):
@@ -381,22 +357,17 @@ def tile_block_pc_kernel(tc, h_attn, norm2_w, ffn_wk, ffn_wv, out):
                 load_wv(g + 3)
 
         last = FF_GROUPS - 1
-        third = open_sums(["bank"] * 3 + ["stage"], PIECE)
+        third = open_sums("bank", PIECE)
         for g in range(FF_GROUPS):
-            if not (g < EARLY):
+            if (g, 2) not in wv_grouped:
                 group_wv(g, 2, on_vector)
-        for g in range(FF_GROUPS - 1):
-            if not (g < EARLY):
                 quantise_wv(g, 2)
-            if g == 4:
+            if g == 6:
                 quantise_k(last)
                 add_to_sums(last, 0, first_half)
             add_to_sums(g, 2, third)
-        if not (last < EARLY):
-            quantise_wv(last, 2)
-        add_to_sums(last, 2, third)
         add_residual_and_store(0, first_half)
-        fourth = open_sums(["sums"] * 4, PIECE)
+        fourth = open_sums("sums", PIECE)
         for g in range(FF_GROUPS):
             if (g, 3) not in wv_grouped:
                 group_wv(g, 3, on_scalar)

@@ -304,12 +304,12 @@ def tile_block_pc_kernel(tc, h_attn, norm2_w, ffn_wk, ffn_wv, out):
         normalise(3)
         turn(3)
         rectify(0, 1)
+        group_wk(1, 0)
+        group_wv(0, 1, on_vector)
         quantise_hn(2)
         multiply_hidden(0, 2)
         group_hn(3)
         rectify(0, 2)
-        group_wk(1, 0)
-        group_wv(0, 1, on_vector)
         quantise_hn(3)
         multiply_hidden(0, 3)
         rectify(0, 3)
@@ -325,32 +325,22 @@ def tile_block_pc_kernel(tc, h_attn, norm2_w, ffn_wk, ffn_wv, out):
             square(g)
             if more:
                 group_wv(g + 1, 0, on_scalar)
-            if more and g > 0:
-                group_wk(g + 1, 0)
-            elif g > 0:
-                for j in range(1, 3):
-                    group_wv(j, 2, on_vector)
+                if g > 0:
+                    group_wk(g + 1, 0)
+                group_wk(g + 1, 1)
+            if g > 0:
+                group_wv(g, 1, on_vector)
+            thirds = range(1, 5) if not more else range(0, 1) if g == 0 else range(0)
+            for j in thirds:
+                group_wv(j, 2, on_vector)
             if g > 0:
                 quantise_k(g - 1)
                 add_to_sums(g - 1, 0, first_half)
-                group_wv(g, 1, on_vector)
-            if more:
-                group_wk(g + 1, 1)
-            else:
-                for j in range(1, 3):
-                    quantise_wv(j, 2)
-                for j in range(3, 6):
-                    group_wv(j, 2, on_vector)
-            quantise_wv(g, 0)
-            if not more:
-                for j in range(3, 6):
-                    quantise_wv(j, 2)
-            if g == 0:
-                group_wv(g, 2, on_vector)
             if more:
                 quantise_wk(g + 1)
-            if g == 0:
-                quantise_wv(g, 2)
+            quantise_wv(g, 0)
+            for j in thirds:
+                quantise_wv(j, 2)
             if g + 3 < FF_GROUPS:
                 for c in range(D_PASSES):
                     load_wk(g + 3, c)
@@ -358,20 +348,20 @@ def tile_block_pc_kernel(tc, h_attn, norm2_w, ffn_wk, ffn_wv, out):
 
         last = FF_GROUPS - 1
         third = open_sums("bank", PIECE)
-        for g in range(FF_GROUPS):
-            if (g, 2) not in wv_grouped:
-                group_wv(g, 2, on_vector)
-                quantise_wv(g, 2)
-            if g == 6:
-                quantise_k(last)
-                add_to_sums(last, 0, first_half)
+        for g in range(5, FF_GROUPS):
+            group_wv(g, 2, on_vector)
+        for g in range(5):
+            add_to_sums(g, 2, third)
+        quantise_k(last)
+        add_to_sums(last, 0, first_half)
+        for g in range(5, FF_GROUPS):
+            quantise_wv(g, 2)
             add_to_sums(g, 2, third)
         add_residual_and_store(0, first_half)
         fourth = open_sums("sums", PIECE)
         for g in range(FF_GROUPS):
-            if (g, 3) not in wv_grouped:
+            if g > 0:
                 group_wv(g, 3, on_scalar)
-            if (g, 3) not in wv_quantised:
                 quantise_wv(g, 3)
             add_to_sums(g, 3, fourth)
             if g == 5:

@@ -39,8 +39,8 @@ def regroup(copy, grouped, rows):
 
 def regroup_units(copy, grouped, rows):
     copy(
-        out=grouped.rearrange("p t m j -> p m j t"),
-        in_=rows.rearrange("p j (m t) -> p m j t", t=PACK),
+        out=grouped.rearrange("p t (b i) j -> p b t j i", i=2),
+        in_=rows.rearrange("p j (b i t) -> p b t j i", t=PACK, i=2),
     )
 
 

@@ -24,6 +24,7 @@ TOK_TILES = TOKENS // P
 D_PASSES = D_MODEL // K_PASS
 FF_GROUPS = D_FF // K_PASS
 BANK = 512
+QUAD = 4
 PIECE = 256
 RUN = 4
 
@@ -57,8 +58,8 @@ def tile_block_pc_kernel(tc, h_attn, norm2_w, ffn_wk, ffn_wv, out):
         grouped = ctx.enter_context(tc.tile_pool(name="grouped", bufs=2))
         quantised = ctx.enter_context(tc.tile_pool(name="quantised", bufs=2))
         work = ctx.enter_context(tc.tile_pool(name="work", bufs=2))
-        results = ctx.enter_context(tc.tile_pool(name="results", bufs=8))
-        psum = ctx.enter_context(tc.psum_pool(name="psum", bufs=4))
+        results = ctx.enter_context(tc.tile_pool(name="results", bufs=1))
+        psum = ctx.enter_context(tc.psum_pool(name="psum", bufs=3))
         ctx.enter_context(tc.manual_schedule())
 
         h_sb = keep.tile([P, TOK_TILES, D_MODEL], BF16)
@@ -93,6 +94,8 @@ def tile_block_pc_kernel(tc, h_attn, norm2_w, ffn_wk, ffn_wv, out):
 
         identity = keep.tile([P, P], F32)
         make_identity(nc, identity[:])
+        identity_bf16 = keep.tile([P, P], BF16)
+        nc.gpsimd.tensor_copy(out=identity_bf16[:], in_=identity[:])
         ones = keep.tile([P, P], BF16)
         nc.vector.memset(ones[:], 1.0)
         eps = keep.tile([P, 1], F32)
@@ -118,7 +121,7 @@ def tile_block_pc_kernel(tc, h_attn, norm2_w, ffn_wk, ffn_wv, out):
 
         def measure(n):
             one = slice(n, n + 1)
-            squares = work.tile([P, D_MODEL], BF16, name="squares")
+            squares = work.tile([P, D_MODEL], BF16, bufs=1, name="squares")
             nc.scalar.activation(out=squares[:], in_=h_sb[:, n, :], func=ACT.Square, accum_out=sum_sq[:, one])
             nc.scalar.activation(
                 out=rms[:, one], in_=sum_sq[:, one], func=ACT.Sqrt, bias=eps[:], scale=1.0 / D_MODEL
@@ -164,7 +167,7 @@ def tile_block_pc_kernel(tc, h_attn, norm2_w, ffn_wk, ffn_wv, out):
 
         def group_wk(g, c):
             if c == 0:
-                wk_grouped[g] = grouped.tile([P, D_PASSES, PACK, P, PACK], BF16, align_bytes=64, name="wk_grouped")
+                wk_grouped[g] = grouped.tile([P, D_PASSES, PACK, P, PACK], BF16, align_bytes=64, tag="wide", name="wk_grouped")
             regroup_units(nc.vector.tensor_copy, wk_grouped[g][:, c], wk_raws[g][:, c])
 
         def quantise_wk(g):
@@ -179,31 +182,77 @@ def tile_block_pc_kernel(tc, h_attn, norm2_w, ffn_wk, ffn_wv, out):
 
         wv_grouped = {}
         wv_quantised = {}
+        stages = {}
 
-        def grouped_wv(g, quarter):
-            if quarter < 2:
-                if (g, 0) not in wv_grouped:
-                    wv_grouped[g, 0] = grouped.tile([P, BANK, PACK], BF16, align_bytes=64, name="wv_half")
-                return wv_grouped[g, 0][:, quarter * PIECE : (quarter + 1) * PIECE, :]
-            if (g, quarter) not in wv_grouped:
-                wv_grouped[g, quarter] = grouped.tile([P, PIECE, PACK], BF16, align_bytes=64, bufs=4, name="wv_quarter")
-            return wv_grouped[g, quarter][:]
+        def half_tile(g):
+            if g not in wv_grouped:
+                wv_grouped[g] = grouped.tile([P, BANK, PACK], BF16, align_bytes=64, name="wv_half")
+            return wv_grouped[g]
 
-        def group_wv(g, quarter, copy):
-            regroup(copy, grouped_wv(g, quarter), wv_raw[:, g, :, quarter * PIECE : (quarter + 1) * PIECE])
+        def group_half(g, quarter, copy):
+            cols = slice(quarter * PIECE, (quarter + 1) * PIECE)
+            regroup(copy, half_tile(g)[:, cols, :], wv_raw[:, g, :, cols])
 
-        def quantise_wv(g, quarter):
-            width = BANK if quarter < 2 else PIECE
-            bufs = {2: FF_GROUPS, 3: 6}.get(quarter, 2)
-            kind = ("half", "half", "third", "fourth")[quarter]
-            codes = quantised.tile([P, width], U32, align_bytes=64, bufs=bufs, name="wv_codes_" + kind)
-            scales = quantised.tile([P, width], U8, align_bytes=64, bufs=bufs, name="wv_scales_" + kind)
+        def stage_half(g):
+            stages[g] = psum.tile([P, PIECE, PACK], BF16, tag="stage", bufs=1, name="stage")
+            for first in range(0, PIECE, P):
+                cols = slice(first, first + P)
+                nc.tensor.matmul(
+                    out=stages[g][:, cols, :].rearrange("p (b i) t -> p b t i", i=8),
+                    lhsT=identity_bf16[:],
+                    rhs=wv_raw[:, g, :, cols].rearrange("p t (b i) -> p b t i", i=8),
+                    start=True,
+                    stop=True,
+                )
+
+        def unstage_half(g):
+            nc.scalar.copy(out=half_tile(g)[:, :PIECE, :], in_=stages[g][:])
+
+        def quantise_half(g):
+            codes = quantised.tile([P, BANK], U32, align_bytes=64, name="half_codes")
+            scales = quantised.tile([P, BANK], U8, align_bytes=64, name="half_scales")
             nc.vector.quantize_mx(
                 out=codes[:].bitcast(FP8X4),
                 scales=scales[:],
-                in_=wv_grouped[g, quarter][:].rearrange("p d t -> p (d t)"),
+                in_=wv_grouped[g][:].rearrange("p d t -> p (d t)"),
             )
-            wv_quantised[g, quarter] = codes, scales
+            wv_quantised[g, 0] = codes[:], scales[:]
+
+        def group_third(groups):
+            wv_grouped[2] = grouped.tile([P, QUAD, PIECE, PACK], BF16, align_bytes=64, tag="wide", name="wv_third")
+            nc.vector.tensor_copy(
+                out=wv_grouped[2][:].rearrange("p g (c i) t -> p g c t i", i=RUN),
+                in_=wv_raw[:, groups, :, 2 * PIECE : 3 * PIECE].rearrange("p g t (c i) -> p g c t i", i=RUN),
+            )
+
+        def quantise_third(groups):
+            codes = quantised.tile([P, QUAD, PIECE], U32, align_bytes=64, name="third_codes")
+            scales = quantised.tile([P, QUAD, PIECE], U8, align_bytes=64, name="third_scales")
+            nc.vector.quantize_mx(
+                out=codes[:].rearrange("p g d -> p (g d)").bitcast(FP8X4),
+                scales=scales[:].rearrange("p g d -> p (g d)"),
+                in_=wv_grouped[2][:].rearrange("p g d t -> p (g d t)"),
+            )
+            for i in range(QUAD):
+                wv_quantised[groups.start + i, 2] = codes[:, i, :], scales[:, i, :]
+
+        def group_fourth(g, copy):
+            if (3, g // 2) not in wv_grouped:
+                wv_grouped[3, g // 2] = grouped.tile(
+                    [P, 2, PIECE, PACK], BF16, align_bytes=64, bufs=3, name="wv_fourth"
+                )
+            regroup(copy, wv_grouped[3, g // 2][:, g % 2], wv_raw[:, g, :, 3 * PIECE :])
+
+        def quantise_fourth(pair):
+            codes = quantised.tile([P, 2, PIECE], U32, align_bytes=64, bufs=3, name="fourth_codes")
+            scales = quantised.tile([P, 2, PIECE], U8, align_bytes=64, bufs=3, name="fourth_scales")
+            nc.vector.quantize_mx(
+                out=codes[:].rearrange("p g d -> p (g d)").bitcast(FP8X4),
+                scales=scales[:].rearrange("p g d -> p (g d)"),
+                in_=wv_grouped[3, pair][:].rearrange("p g d t -> p (g d t)"),
+            )
+            for i in range(2):
+                wv_quantised[2 * pair + i, 3] = codes[:, i, :], scales[:, i, :]
 
         k_codes = keep.tile([P, FF_GROUPS, TOKENS], U32, align_bytes=64)
         k_scales = keep.tile([P, FF_GROUPS, TOKENS], U8, align_bytes=64)
@@ -248,8 +297,11 @@ def tile_block_pc_kernel(tc, h_attn, norm2_w, ffn_wk, ffn_wv, out):
                 in_=k_grouped[g][:].rearrange("p k t -> p (k t)"),
             )
 
-        def open_sums(tag, width):
-            return [psum.tile([P, width], F32, tag=tag, name="sums%d" % n) for n in range(TOK_TILES)]
+        def open_sums(tags, width):
+            bufs = {"sums": 4, "bank": 3, "stage": 1}
+            return [
+                psum.tile([P, width], F32, tag=tag, bufs=bufs[tag], name="sums%d" % n) for n, tag in enumerate(tags)
+            ]
 
         def add_to_sums(g, quarter, sums):
             codes, scales = wv_quantised[g, quarter]
@@ -259,8 +311,8 @@ def tile_block_pc_kernel(tc, h_attn, norm2_w, ffn_wk, ffn_wv, out):
                     out=sums[n][:],
                     lhsT=k_codes[:, g, toks].bitcast(FP8X4),
                     lhsT_scale=k_scales[:, g, toks],
-                    rhs=codes[:].bitcast(FP8X4),
-                    rhs_scale=scales[:],
+                    rhs=codes.bitcast(FP8X4),
+                    rhs_scale=scales,
                     start=(g == 0),
                     stop=(g == FF_GROUPS - 1),
                 )
@@ -269,11 +321,12 @@ def tile_block_pc_kernel(tc, h_attn, norm2_w, ffn_wk, ffn_wv, out):
             width = sums[0].shape[1]
             cols = slice(quarter * PIECE, quarter * PIECE + width)
             for n in range(TOK_TILES):
-                result = results.tile([P, BANK], F32, name="result")
+                bufs = TOK_TILES if width == BANK else 2 * TOK_TILES
+                result = results.tile([P, width], F32, bufs=bufs, name="result%d" % width)
                 nc.vector.tensor_tensor(
-                    out=result[:, :width], in0=sums[n][:], in1=h_sb[:, n, cols], op=ALU.add
+                    out=result[:], in0=sums[n][:], in1=h_sb[:, n, cols], op=ALU.add
                 )
-                nc.sync.dma_start(out=out_rows[n][:, cols], in_=result[:, :width])
+                nc.sync.dma_start(out=out_rows[n][:, cols], in_=result[:])
 
         on_scalar = nc.scalar.copy
         on_vector = nc.vector.tensor_copy
@@ -291,21 +344,21 @@ def tile_block_pc_kernel(tc, h_attn, norm2_w, ffn_wk, ffn_wv, out):
         measure(3)
         group_hn(1)
         quantise_hn(0)
-        group_wv(0, 0, on_scalar)
+        group_half(0, 0, on_scalar)
         quantise_wk(0)
         multiply_hidden(0, 0)
         normalise(2)
         turn(2)
         quantise_hn(1)
         multiply_hidden(0, 1)
-        group_wv(0, 3, on_scalar)
+        group_fourth(0, on_scalar)
         group_hn(2)
         rectify(0, 0)
         normalise(3)
         turn(3)
         rectify(0, 1)
         group_wk(1, 0)
-        group_wv(0, 1, on_vector)
+        group_half(0, 1, on_vector)
         quantise_hn(2)
         multiply_hidden(0, 2)
         group_hn(3)
@@ -313,57 +366,62 @@ def tile_block_pc_kernel(tc, h_attn, norm2_w, ffn_wk, ffn_wv, out):
         quantise_hn(3)
         multiply_hidden(0, 3)
         rectify(0, 3)
-        quantise_wv(0, 3)
 
-        first_half = open_sums("sums", BANK)
+        first_half = open_sums(["sums"] * 4, BANK)
         for g in range(FF_GROUPS):
             more = g + 1 < FF_GROUPS
             if g > 0:
                 for n in range(TOK_TILES):
                     multiply_hidden(g, n)
                     rectify(g, n)
+            if more:
+                stage_half(g + 1)
             square(g)
             if more:
-                group_wv(g + 1, 0, on_scalar)
+                unstage_half(g + 1)
+                if (g + 1) % 3 == 2:
+                    group_half(g + 1, 1, on_scalar)
                 if g > 0:
                     group_wk(g + 1, 0)
                 group_wk(g + 1, 1)
-            if g > 0:
-                group_wv(g, 1, on_vector)
-            thirds = range(1, 5) if not more else range(0, 1) if g == 0 else range(0)
-            for j in thirds:
-                group_wv(j, 2, on_vector)
+            if g > 0 and g % 3 < 2:
+                group_half(g, 1, on_vector)
+            if not more:
+                group_third(slice(0, QUAD))
             if g > 0:
                 quantise_k(g - 1)
                 add_to_sums(g - 1, 0, first_half)
             if more:
                 quantise_wk(g + 1)
-            quantise_wv(g, 0)
-            for j in thirds:
-                quantise_wv(j, 2)
+            quantise_half(g)
             if g + 3 < FF_GROUPS:
                 for c in range(D_PASSES):
                     load_wk(g + 3, c)
                 load_wv(g + 3)
 
         last = FF_GROUPS - 1
-        third = open_sums("bank", PIECE)
-        for g in range(5, FF_GROUPS):
-            group_wv(g, 2, on_vector)
-        for g in range(5):
+        third = open_sums(["bank"] * 3 + ["stage"], PIECE)
+        quantise_third(slice(0, QUAD))
+        group_third(slice(QUAD, FF_GROUPS))
+        for g in range(QUAD):
             add_to_sums(g, 2, third)
         quantise_k(last)
         add_to_sums(last, 0, first_half)
-        for g in range(5, FF_GROUPS):
-            quantise_wv(g, 2)
+        quantise_third(slice(QUAD, FF_GROUPS))
+        for g in range(QUAD, FF_GROUPS):
             add_to_sums(g, 2, third)
+        group_fourth(last, on_vector)
+        group_fourth(1, on_scalar)
+        quantise_fourth(0)
         add_residual_and_store(0, first_half)
-        fourth = open_sums("sums", PIECE)
-        for g in range(FF_GROUPS):
-            if g > 0:
-                group_wv(g, 3, on_scalar)
-                quantise_wv(g, 3)
-            add_to_sums(g, 3, fourth)
-            if g == 5:
-                add_residual_and_store(2, third)
+        fourth = open_sums(["sums"] * 4, PIECE)
+        for pair in range(FF_GROUPS // 2):
+            if pair > 0:
+                group_fourth(2 * pair, on_scalar)
+                if 2 * pair + 1 < last:
+                    group_fourth(2 * pair + 1, on_scalar)
+                quantise_fourth(pair)
+            for g in (2 * pair, 2 * pair + 1):
+                add_to_sums(g, 3, fourth)
+        add_residual_and_store(2, third)
         add_residual_and_store(3, fourth)

@@ -26,6 +26,7 @@ FF_GROUPS = D_FF // K_PASS
 BANK = 512
 QUAD = 4
 PIECE = 256
+SHARE = 64
 RUN = 4
 
 FLOPS = 2 * 2 * TOKENS * D_MODEL * D_FF
@@ -101,11 +102,10 @@ def tile_block_pc_kernel(tc, h_attn, norm2_w, ffn_wk, ffn_wv, out):
         eps = keep.tile([P, 1], F32)
         nc.vector.memset(eps[:], EPS)
         table_warm = keep.tile([P, 1], F32)
-        nc.scalar.activation(out=table_warm[:], in_=eps[:], func=ACT.Sqrt)
+        nc.scalar.activation(out=table_warm[:], in_=eps[:], func=ACT.Abs_reciprocal_sqrt)
 
         gain = keep.tile([P, D_MODEL], BF16)
         sum_sq = keep.tile([P, TOK_TILES], F32)
-        rms = keep.tile([P, TOK_TILES], F32)
         inv_rms = keep.tile([P, TOK_TILES], F32)
         hn_codes = keep.tile([P, TOK_TILES, D_PASSES, P], U32, align_bytes=64)
         hn_scales = keep.tile([P, TOK_TILES, D_PASSES, P], U8, align_bytes=64)
@@ -124,12 +124,11 @@ def tile_block_pc_kernel(tc, h_attn, norm2_w, ffn_wk, ffn_wv, out):
             squares = work.tile([P, D_MODEL], BF16, bufs=1, name="squares")
             nc.scalar.activation(out=squares[:], in_=h_sb[:, n, :], func=ACT.Square, accum_out=sum_sq[:, one])
             nc.scalar.activation(
-                out=rms[:, one], in_=sum_sq[:, one], func=ACT.Sqrt, bias=eps[:], scale=1.0 / D_MODEL
+                out=inv_rms[:, one], in_=sum_sq[:, one], func=ACT.Abs_reciprocal_sqrt, bias=eps[:], scale=1.0 / D_MODEL
             )
 
         def normalise(n):
             one = slice(n, n + 1)
-            nc.vector.reciprocal(out=inv_rms[:, one], in_=rms[:, one])
             hn_tiles[n] = work.tile([P, D_MODEL], BF16, name="hn")
             nc.vector.scalar_tensor_tensor(
                 out=hn_tiles[n][:],
@@ -189,8 +188,7 @@ def tile_block_pc_kernel(tc, h_attn, norm2_w, ffn_wk, ffn_wv, out):
                 wv_grouped[g] = grouped.tile([P, BANK, PACK], BF16, align_bytes=64, name="wv_half")
             return wv_grouped[g]
 
-        def group_half(g, quarter, copy):
-            cols = slice(quarter * PIECE, (quarter + 1) * PIECE)
+        def group_half(g, cols, copy):
             regroup(copy, half_tile(g)[:, cols, :], wv_raw[:, g, :, cols])
 
         def stage_half(g):
@@ -344,7 +342,7 @@ def tile_block_pc_kernel(tc, h_attn, norm2_w, ffn_wk, ffn_wv, out):
         measure(3)
         group_hn(1)
         quantise_hn(0)
-        group_half(0, 0, on_scalar)
+        group_half(0, slice(0, PIECE), on_scalar)
         quantise_wk(0)
         multiply_hidden(0, 0)
         normalise(2)
@@ -358,7 +356,7 @@ def tile_block_pc_kernel(tc, h_attn, norm2_w, ffn_wk, ffn_wv, out):
         turn(3)
         rectify(0, 1)
         group_wk(1, 0)
-        group_half(0, 1, on_vector)
+        group_half(0, slice(PIECE, BANK), on_vector)
         quantise_hn(2)
         multiply_hidden(0, 2)
         group_hn(3)
@@ -379,13 +377,12 @@ def tile_block_pc_kernel(tc, h_attn, norm2_w, ffn_wk, ffn_wv, out):
             square(g)
             if more:
                 unstage_half(g + 1)
-                if (g + 1) % 3 == 2:
-                    group_half(g + 1, 1, on_scalar)
+                group_half(g + 1, slice(PIECE, PIECE + SHARE), on_scalar)
                 if g > 0:
                     group_wk(g + 1, 0)
                 group_wk(g + 1, 1)
-            if g > 0 and g % 3 < 2:
-                group_half(g, 1, on_vector)
+            if g > 0:
+                group_half(g, slice(PIECE + SHARE, BANK), on_vector)
             if not more:
                 group_third(slice(0, QUAD))
             if g > 0:

@@ -301,9 +301,9 @@ def tile_block_pc_kernel(tc, h_attn, norm2_w, ffn_wk, ffn_wv, out):
                 psum.tile([P, width], F32, tag=tag, bufs=bufs[tag], name="sums%d" % n) for n, tag in enumerate(tags)
             ]
 
-        def add_to_sums(g, quarter, sums):
+        def add_to_sums(g, quarter, sums, tiles=range(TOK_TILES)):
             codes, scales = wv_quantised[g, quarter]
-            for n in range(TOK_TILES):
+            for n in tiles:
                 toks = slice(n * P, (n + 1) * P)
                 nc.tensor.matmul_mx(
                     out=sums[n][:],
@@ -407,17 +407,17 @@ def tile_block_pc_kernel(tc, h_attn, norm2_w, ffn_wk, ffn_wv, out):
         quantise_third(slice(QUAD, FF_GROUPS))
         for g in range(QUAD, FF_GROUPS):
             add_to_sums(g, 2, third)
-        group_fourth(last, on_vector)
         group_fourth(1, on_scalar)
         quantise_fourth(0)
         add_residual_and_store(0, first_half)
         fourth = open_sums(["sums"] * 4, PIECE)
-        for pair in range(FF_GROUPS // 2):
-            if pair > 0:
-                group_fourth(2 * pair, on_scalar)
-                if 2 * pair + 1 < last:
-                    group_fourth(2 * pair + 1, on_scalar)
-                quantise_fourth(pair)
+        for n in range(TOK_TILES):
+            for g in range(2):
+                add_to_sums(g, 3, fourth, tiles=(n,))
+        for pair in range(1, FF_GROUPS // 2):
+            group_fourth(2 * pair, on_scalar)
+            group_fourth(2 * pair + 1, on_scalar if 2 * pair + 1 < last else on_vector)
+            quantise_fourth(pair)
             for g in (2 * pair, 2 * pair + 1):
                 add_to_sums(g, 3, fourth)
         add_residual_and_store(2, third)

from contextlib import ExitStack

import concourse.mybir as mybir
from concourse.masks import make_identity

F32 = mybir.dt.float32
BF16 = mybir.dt.bfloat16
U32 = mybir.dt.uint32
U8 = mybir.dt.uint8
FP8X4 = mybir.dt.float8_e4m3fn_x4
ACT = mybir.ActivationFunctionType
ALU = mybir.AluOpType

P = 128
PACK = 4
K_PASS = P * PACK

TOKENS = 512
D_MODEL = 1024
D_FF = 4096
EPS = 1e-5

TOK_TILES = TOKENS // P
D_PASSES = D_MODEL // K_PASS
FF_GROUPS = D_FF // K_PASS
BANK = 512
QUAD = 4
PIECE = 256
SHARE = 64
RUN = 4

FLOPS = 2 * 2 * TOKENS * D_MODEL * D_FF


def regroup(copy, grouped, rows):
    copy(
        out=grouped.rearrange("p (c i) t -> p c t i", i=RUN),
        in_=rows.rearrange("p t (c i) -> p c t i", i=RUN),
    )


def regroup_units(copy, grouped, rows):
    copy(
        out=grouped.rearrange("p t (b i) j -> p b t j i", i=2),
        in_=rows.rearrange("p j (b i t) -> p b t j i", t=PACK, i=2),
    )


def tile_block_pc_kernel(tc, h_attn, norm2_w, ffn_wk, ffn_wv, out):
    nc = tc.nc
    h_rows = h_attn.flatten_outer_dims().rearrange("(n p) d -> n p d", p=P)
    out_rows = out.flatten_outer_dims().rearrange("(n p) d -> n p d", p=P)
    wk_rows = ffn_wk.rearrange("(c p t) f -> c p t f", t=PACK, p=P)
    wv_rows = ffn_wv.rearrange("(g p t) d -> g p t d", t=PACK, p=P)

    with ExitStack() as ctx:
        keep = ctx.enter_context(tc.tile_pool(name="keep", bufs=1))
        wk_loads = ctx.enter_context(tc.tile_pool(name="wk_loads", bufs=3))
        grouped = ctx.enter_context(tc.tile_pool(name="grouped", bufs=2))
        quantised = ctx.enter_context(tc.tile_pool(name="quantised", bufs=2))
        work = ctx.enter_context(tc.tile_pool(name="work", bufs=2))
        results = ctx.enter_context(tc.tile_pool(name="results", bufs=1))
        psum = ctx.enter_context(tc.psum_pool(name="psum", bufs=3))
        ctx.enter_context(tc.manual_schedule())

        h_sb = keep.tile([P, TOK_TILES, D_MODEL], BF16)
        wv_raw = keep.tile([P, FF_GROUPS, PACK, D_MODEL], BF16)
        gain_row = keep.tile([P, D_MODEL], BF16)
        nc.vector.memset(gain_row[:].bitcast(U32), 0)
        wk_raws = {}

        def load_h(n):
            nc.sync.dma_start(out=h_sb[:, n, :], in_=h_rows[n])

        def load_wk(g, c):
            if c == 0:
                wk_raws[g] = wk_loads.tile([P, D_PASSES, PACK, K_PASS], BF16, name="wk_raw")
            nc.sync.dma_start(out=wk_raws[g][:, c], in_=wk_rows[c, :, :, g * K_PASS : (g + 1) * K_PASS])

        def load_wv(g):
            nc.sync.dma_start(out=wv_raw[:, g], in_=wv_rows[g])

        load_h(0)
        load_wk(0, 0)
        nc.sync.dma_start(out=gain_row[0:1, :], in_=norm2_w.rearrange("(o d) -> o d", o=1))
        load_h(1)
        load_wk(0, 1)
        load_h(2)
        load_h(3)
        load_wv(0)
        for g in range(1, 3):
            for c in range(D_PASSES):
                load_wk(g, c)
            load_wv(g)

        identity = keep.tile([P, P], F32)
        make_identity(nc, identity[:])
        identity_bf16 = keep.tile([P, P], BF16)
        nc.gpsimd.tensor_copy(out=identity_bf16[:], in_=identity[:])
        ones = keep.tile([P, P], BF16)
        nc.vector.memset(ones[:], 1.0)
        eps = keep.tile([P, 1], F32)
        nc.vector.memset(eps[:], EPS)
        table_warm = keep.tile([P, 1], F32)
        nc.scalar.activation(out=table_warm[:], in_=eps[:], func=ACT.Abs_reciprocal_sqrt)

        gain = keep.tile([P, D_MODEL], BF16)
        sum_sq = keep.tile([P, TOK_TILES], F32)
        inv_rms = keep.tile([P, TOK_TILES], F32)
        hn_codes = keep.tile([P, TOK_TILES, D_PASSES, P], U32, align_bytes=64)
        hn_scales = keep.tile([P, TOK_TILES, D_PASSES, P], U8, align_bytes=64)
        hn_tiles = {}
        hn_banks = {}

        def spread_gain():
            gain_ps = psum.tile([P, D_MODEL], BF16, tag="bank", name="gain_ps")
            for first in range(0, D_MODEL, BANK):
                cols = slice(first, first + BANK)
                nc.tensor.matmul(out=gain_ps[:, cols], lhsT=ones[:], rhs=gain_row[:, cols], start=True, stop=True)
            nc.vector.tensor_copy(out=gain[:], in_=gain_ps[:])

        def measure(n):
            one = slice(n, n + 1)
            squares = work.tile([P, D_MODEL], BF16, bufs=1, name="squares")
            nc.scalar.activation(out=squares[:], in_=h_sb[:, n, :], func=ACT.Square, accum_out=sum_sq[:, one])
            nc.scalar.activation(
                out=inv_rms[:, one], in_=sum_sq[:, one], func=ACT.Abs_reciprocal_sqrt, bias=eps[:], scale=1.0 / D_MODEL
            )

        def normalise(n):
            one = slice(n, n + 1)
            hn_tiles[n] = work.tile([P, D_MODEL], BF16, name="hn")
            nc.vector.scalar_tensor_tensor(
                out=hn_tiles[n][:],
                in0=h_sb[:, n, :],
                scalar=inv_rms[:, one],
                in1=gain[:],
                op0=ALU.mult,
                op1=ALU.mult,
            )

        def turn(n):
            words = hn_tiles[n][:].bitcast(F32)
            hn_banks[n] = psum.tile([P, D_PASSES, 2, P], F32, tag="bank", name="hn_bank")
            for c in range(D_PASSES):
                for u in range(2):
                    pairs = slice(c * 2 * P + u, (c + 1) * 2 * P, 2)
                    nc.tensor.transpose(hn_banks[n][:, c, u, :], words[:, pairs], identity[:])

        def group_hn(n):
            hn_tiles[n] = work.tile([P, D_PASSES, P, PACK], BF16, align_bytes=64, name="hn_grouped")
            nc.scalar.copy(
                out=hn_tiles[n][:].rearrange("p c k t -> p (c k t)").bitcast(F32).rearrange("p (c k u) -> p c k u", c=D_PASSES, u=2),
                in_=hn_banks[n][:].rearrange("p c u k -> p c k u"),
            )

        def quantise_hn(n):
            nc.vector.quantize_mx(
                out=hn_codes[:, n].rearrange("p c k -> p (c k)").bitcast(FP8X4),
                scales=hn_scales[:, n].rearrange("p c k -> p (c k)"),
                in_=hn_tiles[n][:].rearrange("p c k t -> p (c k t)"),
            )

        wk_grouped = {}
        wk_quantised = {}

        def group_wk(g, c):
            if c == 0:
                wk_grouped[g] = grouped.tile([P, D_PASSES, PACK, P, PACK], BF16, align_bytes=64, tag="wide", name="wk_grouped")
            regroup_units(nc.vector.tensor_copy, wk_grouped[g][:, c], wk_raws[g][:, c])

        def quantise_wk(g):
            codes = quantised.tile([P, D_PASSES, K_PASS], U32, align_bytes=64, name="wk_codes")
            scales = quantised.tile([P, D_PASSES, K_PASS], U8, align_bytes=64, name="wk_scales")
            nc.vector.quantize_mx(
                out=codes[:].rearrange("p c f -> p (c f)").bitcast(FP8X4),
                scales=scales[:].rearrange("p c f -> p (c f)"),
                in_=wk_grouped[g][:].rearrange("p c t m j -> p (c t m j)"),
            )
            wk_quantised[g] = codes, scales

        wv_grouped = {}
        wv_quantised = {}
        stages = {}

        def half_tile(g):
            if g not in wv_grouped:
                wv_grouped[g] = grouped.tile([P, BANK, PACK], BF16, align_bytes=64, name="wv_half")
            return wv_grouped[g]

        def group_half(g, cols, copy):
            regroup(copy, half_tile(g)[:, cols, :], wv_raw[:, g, :, cols])

        def stage_half(g):
            stages[g] = psum.tile([P, PIECE, PACK], BF16, tag="stage", bufs=1, name="stage")
            for first in range(0, PIECE, P):
                cols = slice(first, first + P)
                nc.tensor.matmul(
                    out=stages[g][:, cols, :].rearrange("p (b i) t -> p b t i", i=8),
                    lhsT=identity_bf16[:],
                    rhs=wv_raw[:, g, :, cols].rearrange("p t (b i) -> p b t i", i=8),
                    start=True,
                    stop=True,
                )

        def unstage_half(g):
            nc.scalar.copy(out=half_tile(g)[:, :PIECE, :], in_=stages[g][:])

        def quantise_half(g):
            codes = quantised.tile([P, BANK], U32, align_bytes=64, name="half_codes")
            scales = quantised.tile([P, BANK], U8, align_bytes=64, name="half_scales")
            nc.vector.quantize_mx(
                out=codes[:].bitcast(FP8X4),
                scales=scales[:],
                in_=wv_grouped[g][:].rearrange("p d t -> p (d t)"),
            )
            wv_quantised[g, 0] = codes[:], scales[:]

        def group_third(groups):
            wv_grouped[2] = grouped.tile([P, QUAD, PIECE, PACK], BF16, align_bytes=64, tag="wide", name="wv_third")
            nc.vector.tensor_copy(
                out=wv_grouped[2][:].rearrange("p g (c i) t -> p g c t i", i=RUN),
                in_=wv_raw[:, groups, :, 2 * PIECE : 3 * PIECE].rearrange("p g t (c i) -> p g c t i", i=RUN),
            )

        def quantise_third(groups):
            codes = quantised.tile([P, QUAD, PIECE], U32, align_bytes=64, name="third_codes")
            scales = quantised.tile([P, QUAD, PIECE], U8, align_bytes=64, name="third_scales")
            nc.vector.quantize_mx(
                out=codes[:].rearrange("p g d -> p (g d)").bitcast(FP8X4),
                scales=scales[:].rearrange("p g d -> p (g d)"),
                in_=wv_grouped[2][:].rearrange("p g d t -> p (g d t)"),
            )
            for i in range(QUAD):
                wv_quantised[groups.start + i, 2] = codes[:, i, :], scales[:, i, :]

        def group_fourth(g, copy):
            if (3, g // 2) not in wv_grouped:
                wv_grouped[3, g // 2] = grouped.tile(
                    [P, 2, PIECE, PACK], BF16, align_bytes=64, bufs=3, name="wv_fourth"
                )
            regroup(copy, wv_grouped[3, g // 2][:, g % 2], wv_raw[:, g, :, 3 * PIECE :])

        def quantise_fourth(pair):
            codes = quantised.tile([P, 2, PIECE], U32, align_bytes=64, bufs=3, name="fourth_codes")
            scales = quantised.tile([P, 2, PIECE], U8, align_bytes=64, bufs=3, name="fourth_scales")
            nc.vector.quantize_mx(
                out=codes[:].rearrange("p g d -> p (g d)").bitcast(FP8X4),
                scales=scales[:].rearrange("p g d -> p (g d)"),
                in_=wv_grouped[3, pair][:].rearrange("p g d t -> p (g d t)"),
            )
            for i in range(2):
                wv_quantised[2 * pair + i, 3] = codes[:, i, :], scales[:, i, :]

        k_codes = keep.tile([P, FF_GROUPS, TOKENS], U32, align_bytes=64)
        k_scales = keep.tile([P, FF_GROUPS, TOKENS], U8, align_bytes=64)
        pre_banks = {}
        relus = {}
        k_grouped = {}

        def multiply_hidden(g, n):
            pre = psum.tile([P, PACK, P], F32, tag="bank", name="pre")
            codes, scales = wk_quantised[g]
            for t in range(PACK):
                units = slice(t * P, (t + 1) * P)
                for c in range(D_PASSES):
                    nc.tensor.matmul_mx(
                        out=pre[:, t, :],
                        lhsT=codes[:, c, units].bitcast(FP8X4),
                        lhsT_scale=scales[:, c, units],
                        rhs=hn_codes[:, n, c, :].bitcast(FP8X4),
                        rhs_scale=hn_scales[:, n, c, :],
                        start=(c == 0),
                        stop=(c == D_PASSES - 1),
                    )
            pre_banks[g, n] = pre

        def rectify(g, n):
            if n == 0:
                relus[g] = work.tile([P, TOKENS, PACK], F32, bufs=1, name="relu")
            nc.scalar.activation(
                out=relus[g][:, n * P : (n + 1) * P, :],
                in_=pre_banks[g, n][:].rearrange("p t k -> p k t"),
                func=ACT.Relu,
            )

        def square(g):
            k_grouped[g] = grouped.tile([P, TOKENS, PACK], BF16, align_bytes=64, name="k_grouped")
            nc.scalar.activation(out=k_grouped[g][:], in_=relus[g][:], func=ACT.Square)

        def quantise_k(g):
            nc.vector.quantize_mx(
                out=k_codes[:, g, :].bitcast(FP8X4),
                scales=k_scales[:, g, :],
                in_=k_grouped[g][:].rearrange("p k t -> p (k t)"),
            )

        def open_sums(tags, width):
            bufs = {"sums": 4, "bank": 3, "stage": 1}
            return [
                psum.tile([P, width], F32, tag=tag, bufs=bufs[tag], name="sums%d" % n) for n, tag in enumerate(tags)
            ]

        def add_to_sums(g, quarter, sums, tiles=range(TOK_TILES)):
            codes, scales = wv_quantised[g, quarter]
            for n in tiles:
                toks = slice(n * P, (n + 1) * P)
                nc.tensor.matmul_mx(
                    out=sums[n][:],
                    lhsT=k_codes[:, g, toks].bitcast(FP8X4),
                    lhsT_scale=k_scales[:, g, toks],
                    rhs=codes.bitcast(FP8X4),
                    rhs_scale=scales,
                    start=(g == 0),
                    stop=(g == FF_GROUPS - 1),
                )

        def add_residual_and_store(quarter, sums):
            width = sums[0].shape[1]
            cols = slice(quarter * PIECE, quarter * PIECE + width)
            for n in range(TOK_TILES):
                bufs = TOK_TILES if width == BANK else 2 * TOK_TILES
                result = results.tile([P, width], F32, bufs=bufs, name="result%d" % width)
                nc.vector.tensor_tensor(
                    out=result[:], in0=sums[n][:], in1=h_sb[:, n, cols], op=ALU.add
                )
                nc.sync.dma_start(out=out_rows[n][:, cols], in_=result[:])

        on_scalar = nc.scalar.copy
        on_vector = nc.vector.tensor_copy
        measure(0)
        group_wk(0, 0)
        spread_gain()
        measure(1)
        normalise(0)
        turn(0)
        group_wk(0, 1)
        measure(2)
        group_hn(0)
        normalise(1)
        turn(1)
        measure(3)
        group_hn(1)
        quantise_hn(0)
        group_half(0, slice(0, PIECE), on_scalar)
        quantise_wk(0)
        multiply_hidden(0, 0)
        normalise(2)
        turn(2)
        quantise_hn(1)
        multiply_hidden(0, 1)
        group_fourth(0, on_scalar)
        group_hn(2)
        rectify(0, 0)
        normalise(3)
        turn(3)
        rectify(0, 1)
        group_wk(1, 0)
        group_half(0, slice(PIECE, BANK), on_vector)
        quantise_hn(2)
        multiply_hidden(0, 2)
        group_hn(3)
        rectify(0, 2)
        quantise_hn(3)
        multiply_hidden(0, 3)
        rectify(0, 3)

        first_half = open_sums(["sums"] * 4, BANK)
        for g in range(FF_GROUPS):
            more = g + 1 < FF_GROUPS
            if g > 0:
                for n in range(TOK_TILES):
                    multiply_hidden(g, n)
                    rectify(g, n)
            if more:
                stage_half(g + 1)
            square(g)
            if more:
                unstage_half(g + 1)
                group_half(g + 1, slice(PIECE, PIECE + SHARE), on_scalar)
                if g > 0:
                    group_wk(g + 1, 0)
                group_wk(g + 1, 1)
            if g > 0:
                group_half(g, slice(PIECE + SHARE, BANK), on_vector)
            if not more:
                group_third(slice(0, QUAD))
            if g > 0:
                quantise_k(g - 1)
                add_to_sums(g - 1, 0, first_half)
            if more:
                quantise_wk(g + 1)
            quantise_half(g)
            if g + 3 < FF_GROUPS:
                for c in range(D_PASSES):
                    load_wk(g + 3, c)
                load_wv(g + 3)

        last = FF_GROUPS - 1
        third = open_sums(["bank"] * 3 + ["stage"], PIECE)
        quantise_third(slice(0, QUAD))
        group_third(slice(QUAD, FF_GROUPS))
        for g in range(QUAD):
            add_to_sums(g, 2, third)
        quantise_k(last)
        add_to_sums(last, 0, first_half)
        quantise_third(slice(QUAD, FF_GROUPS))
        for g in range(QUAD, FF_GROUPS):
            add_to_sums(g, 2, third)
        group_fourth(1, on_scalar)
        quantise_fourth(0)
        add_residual_and_store(0, first_half)
        fourth = open_sums(["sums"] * 4, PIECE)
        for n in range(TOK_TILES):
            for g in range(2):
                add_to_sums(g, 3, fourth, tiles=(n,))
        for pair in range(1, FF_GROUPS // 2):
            group_fourth(2 * pair, on_scalar)
            group_fourth(2 * pair + 1, on_scalar if 2 * pair + 1 < last else on_vector)
            quantise_fourth(pair)
            for g in (2 * pair, 2 * pair + 1):
                add_to_sums(g, 3, fourth)
        add_residual_and_store(2, third)
        add_residual_and_store(3, fourth)
